import numpy as np
import ml_dtypes


def mxq(x, axis, fmt="e4m3"):
    dtype, down = {"e4m3": (ml_dtypes.float8_e4m3fn, 7), "e5m2": (ml_dtypes.float8_e5m2, 14)}[fmt]
    v = np.moveaxis(np.asarray(x, np.float32).astype(ml_dtypes.bfloat16).astype(np.float64), axis, -1)
    blocks = v.reshape(v.shape[:-1] + (-1, 32))
    amax = np.abs(blocks).max(-1, keepdims=True)
    byte = np.maximum(np.where(amax > 0, np.frexp(amax)[1] - 1 + 127, 0) - down, 1)
    scale = np.exp2(byte - 127.0)
    codes = (blocks / scale).astype(np.float32).astype(dtype).astype(np.float64)
    return np.moveaxis((codes * scale).reshape(v.shape), -1, axis)


WIDE = False


def mx_kscale(k):
    if not WIDE:
        return np.ones(k)
    levels = np.array([10, -10, 5, -5, 0])
    if k % 512:
        return np.exp2(np.random.permutation(np.resize(levels, k // 32))).repeat(32)
    a = np.empty((k // 512, 16))
    for p in range(k // 512):
        a[p, :8] = np.random.permutation(np.resize(levels, 8))
        for g in range(8):
            far = levels[np.abs(levels - a[p, g]) >= 10]
            a[p, g + 8] = far[np.random.randint(len(far))]
    return np.exp2(a.ravel()).repeat(32)


BF16 = ml_dtypes.bfloat16


def bf(x):
    return np.asarray(x, np.float32).astype(BF16)


def f64(x):
    return np.asarray(x).astype(np.float64)


E2M1 = np.array([0.0, 0.5, 1.0, 1.5, 2.0, 3.0, 4.0, 6.0, -0.0, -0.5, -1.0, -1.5, -2.0, -3.0, -4.0, -6.0])


def pack_weight(w, fmt):
    k, n = w.shape
    w = f64(bf(w)).reshape(k // 32, 32, n)
    amax = np.abs(w).max(1)
    if fmt == "e4m3":
        byte = np.frexp(amax)[1] - 1 + 127 - 7
    else:
        mant, ex = np.frexp(amax / 6.0)
        byte = np.where(mant > 0.5, ex, ex - 1) + 127
    byte = np.clip(np.where(amax > 0, byte, 1), 1, 254)
    scaled = (w * np.exp2(127.0 - byte)[:, None, :]).reshape(k, n).astype(np.float32)
    by_word = np.ascontiguousarray(scaled.reshape(k // 512, 128, 4, n).transpose(0, 1, 3, 2))
    if fmt == "e4m3":
        words = by_word.astype(ml_dtypes.float8_e4m3fn).view(np.uint8)
    else:
        c = by_word.astype(ml_dtypes.float4_e2m1fn).view(np.uint8) & 0xF
        words = c[..., 0::2] | (c[..., 1::2] << 4)
    return np.ascontiguousarray(words), np.ascontiguousarray(byte.astype(np.uint8).reshape(k // 512, 16, n))


def unpack_weight(words, scales, fmt):
    g, p, n, _ = words.shape
    if fmt == "e4m3":
        vals = np.ascontiguousarray(words).view(ml_dtypes.float8_e4m3fn).astype(np.float64)
    else:
        nib = np.empty((g, p, n, 4), np.uint8)
        nib[..., 0::2] = words & 0xF
        nib[..., 1::2] = words >> 4
        vals = E2M1[nib]
    vals = vals * np.repeat(np.exp2(scales.astype(np.float64) - 127.0), 8, axis=1)[..., None]
    return vals.transpose(0, 1, 3, 2).reshape(g * 512, n)
def pack4(w):
    words, scales = pack_weight(w, "e2m1")
    return words.reshape(words.shape[0], 128, -1), scales


def unpack4(words, scales):
    return unpack_weight(words.reshape(words.shape[0], 128, -1, 2), scales, "e2m1")


B, N, D, F1, F2, F3, G1, G2 = 4, 32, 512, 512, 1024, 512, 512, 512
ALPHA = 0.2


def lrelu(v):
    return np.maximum(v, ALPHA * v)


def draw0():
    s, t = mx_kscale(D), mx_kscale(F1)
    ss = np.concatenate([s, s])
    x = bf(np.random.standard_normal((B, N, D)) * s)
    fe_w0_words, fe_w0_scales = pack4(np.random.standard_normal((D + D, F1)) / np.sqrt(D + D) / ss[:, None] * t)
    fe_b0 = bf(np.random.standard_normal(F1) * 0.3 * t)
    fe_w1_words, fe_w1_scales = pack4(np.random.standard_normal((F1, F2)) * 1.4 / np.sqrt(F1) / t[:, None])
    fe_b1 = bf(np.random.standard_normal(F2) * 0.3)
    return {"x": x,
            "fe_w0_words": fe_w0_words,
            "fe_w0_scales": fe_w0_scales,
            "fe_b0": fe_b0,
            "fe_w1_words": fe_w1_words,
            "fe_w1_scales": fe_w1_scales,
            "fe_b1": fe_b1}


def core(x, fe_w0_words, fe_w0_scales, fe_b0, fe_w1_words, fe_w1_scales, fe_b1):
    xq = mxq(f64(x), 2, "e4m3")
    w0 = unpack4(fe_w0_words, fe_w0_scales)
    u = xq @ w0[:D]
    v = xq @ w0[D:]
    e1 = lrelu(u[:, :, None, :] + v[:, None, :, :] + f64(fe_b0))
    return lrelu((mxq(e1, 3, "e4m3") @ unpack4(fe_w1_words, fe_w1_scales)) + f64(fe_b1))


def e4m3fn_bytes(y):
    return np.clip(np.asarray(y, np.float64), -448.0, 448.0).astype(np.float32).astype(ml_dtypes.float8_e4m3fn).view(np.uint8)


def e4m3fn_values(b):
    return np.asarray(b, np.uint8).view(ml_dtypes.float8_e4m3fn).astype(np.float64)


def setup_inputs():
    d = draw0()
    x0 = np.asarray(d['x']).astype(np.float64)
    s = (np.max(np.abs(x0), axis=(0, 1), keepdims=True) / 448.0).astype(np.float32)
    out = {}
    for k, v in d.items():
        if k == 'x':
            out['x_bytes'] = e4m3fn_bytes(x0 / s.astype(np.float64))
            out['x_scale'] = s
        else:
            out[k] = v
    return out


def reference(x_bytes, x_scale, fe_w0_words, fe_w0_scales, fe_b0, fe_w1_words, fe_w1_scales, fe_b1):
    return core(e4m3fn_values(x_bytes) * x_scale.astype(np.float64), fe_w0_words, fe_w0_scales, fe_b0, fe_w1_words, fe_w1_scales, fe_b1)

@@ -1,0 +1,204 @@
+from contextlib import ExitStack
+
+import concourse.mybir as mybir
+from concourse.masks import make_identity
+
+B, N, D, F1, F2 = 4, 32, 512, 512, 1024
+FLOPS = 2 * 2 * B * N * D * F1 + 2 * B * N * N * F1 * F2
+
+F32 = mybir.dt.float32
+BF16 = mybir.dt.bfloat16
+U32 = mybir.dt.uint32
+I32 = mybir.dt.int32
+U8 = mybir.dt.uint8
+E4M3 = mybir.dt.float8_e4m3fn
+FP8X4 = mybir.dt.float8_e4m3fn_x4
+FP4X4 = mybir.dt.float4_e2m1fn_x4
+ALU = mybir.AluOpType
+ACT = mybir.ActivationFunctionType
+
+P = 128
+ALPHA = 0.2
+V_ROUTE = (3, 11, 19, 27)
+
+
+def tile_graph_gan_pa_w4_kernel(tc, x_bytes, x_scale, fe_w0_words, fe_w0_scales, fe_b0, fe_w1_words, fe_w1_scales, fe_b1, out):
+    nc = tc.nc
+    with ExitStack() as ctx:
+        keep = ctx.enter_context(tc.tile_pool(name="keep", bufs=1))
+        xp = ctx.enter_context(tc.tile_pool(name="xp", bufs=2))
+        uvp = ctx.enter_context(tc.tile_pool(name="uvp", bufs=2))
+        zp = ctx.enter_context(tc.tile_pool(name="zp", bufs=3))
+        gp = ctx.enter_context(tc.tile_pool(name="gp", bufs=2))
+        op = ctx.enter_context(tc.tile_pool(name="op", bufs=4))
+        psz = ctx.enter_context(tc.psum_pool(name="psz", bufs=3))
+        psa = ctx.enter_context(tc.psum_pool(name="psa", bufs=5))
+
+        xb = keep.tile([P, D], U8, name="xb", align_bytes=64)
+        nc.sync.dma_start(out=xb[:], in_=x_bytes.rearrange("b n k -> (b n) k"))
+        xsc = keep.tile([P, 4], F32, name="xsc")
+        nc.sync.dma_start(out=xsc[:], in_=x_scale.rearrange("o q (p t) -> p (o q t)", t=4))
+        w0 = keep.tile([P, 2, 2 * F1], U8, name="w0", align_bytes=64)
+        nc.sync.dma_start(
+            out=w0[:].rearrange("p g n -> p (g n)").bitcast(I32).rearrange("p (g n) -> p g n", g=2),
+            in_=fe_w0_words.bitcast(I32).rearrange("g p n -> p g n"),
+        )
+        w0s = keep.tile([P, 2, F1], U8, name="w0s", align_bytes=64)
+        w0s_i = w0s[:].rearrange("p g n -> p (g n)").bitcast(I32)
+        nc.vector.memset(w0s_i, 0)
+        w1s = keep.tile([P, F2], U8, name="w1s", align_bytes=64)
+        nc.vector.memset(w1s[:].bitcast(I32), 0)
+        for q in range(4):
+            nc.sync.dma_start(
+                out=w0s_i.rearrange("p (g n) -> p g n", g=2)[32 * q : 32 * q + 4],
+                in_=fe_w0_scales.bitcast(I32)[:, 4 * q : 4 * q + 4, :].rearrange("g r n -> r g n"),
+            )
+        b0 = keep.tile([P, F1], BF16, name="b0")
+        nc.sync.dma_start(out=b0[:], in_=fe_b0.partition_broadcast(P))
+        w1 = keep.tile([P, 2 * F2], U8, name="w1", align_bytes=64)
+        nc.sync.dma_start(out=w1[:].bitcast(I32), in_=fe_w1_words.bitcast(I32)[0])
+        for q in range(4):
+            nc.sync.dma_start(
+                out=w1s[:].bitcast(I32)[32 * q : 32 * q + 4],
+                in_=fe_w1_scales.bitcast(I32)[0, 4 * q : 4 * q + 4, :],
+            )
+        b1 = keep.tile([P, F2], BF16, name="b1")
+        nc.sync.dma_start(out=b1[:], in_=fe_b1.partition_broadcast(P))
+
+        warm = keep.tile([P, 1], F32, name="warm")
+        nc.vector.memset(warm[:], 0.0)
+        nc.scalar.activation(out=warm[:], in_=warm[:], func=ACT.Relu)
+
+        identb = keep.tile([P, P], BF16, name="identb")
+        make_identity(nc, identb[:])
+        ident = keep.tile([P, P], F32, name="ident")
+        make_identity(nc, ident[:])
+        pi_u = keep.tile([P, P], F32, name="pi_u", align_bytes=64)
+        nc.vector.tensor_copy(
+            out=pi_u[:].rearrange("p (h j l) -> p h j l", h=8, j=4),
+            in_=ident[:].rearrange("p (j h l) -> p h j l", h=8, j=4),
+        )
+        pi_v = keep.tile([P, 2, P], F32, name="pi_v", align_bytes=64)
+        for i in range(2):
+            nc.vector.tensor_copy(
+                out=pi_v[:, i, :].rearrange("p (h j l) -> p h j l", h=8, j=4),
+                in_=ident[:].rearrange("p (l h j) -> p h j l", h=8, j=4),
+            )
+        pi_v2 = pi_v[:].rearrange("p i e -> p (i e)")
+
+        xw = keep.tile([P, D], BF16, name="xw", align_bytes=64)
+        nc.vector.tensor_copy(out=xw[:], in_=xb[:].bitcast(E4M3))
+        xt = psz.tile([P, 4, P], BF16, name="xt", tag="z")
+        for t in range(4):
+            nc.tensor.transpose(xt[:, t, :], xw[:].rearrange("p (k t) -> p t k", t=4)[:, t, :], identb[:])
+
+        def node_products(b):
+            xg = xp.tile([P, 4, N, 4], BF16, name="xg", align_bytes=64)
+            nc.vector.tensor_tensor(
+                out=xg[:],
+                in0=xt[:].rearrange("p t m -> p m t")[:, b * N : (b + 1) * N, :].unsqueeze(1).to_broadcast([P, 4, N, 4]),
+                in1=xsc[:].unsqueeze(1).unsqueeze(1).to_broadcast([P, 4, N, 4]),
+                op=ALU.mult,
+            )
+            xc = xp.tile([P, P], U32, name="xc", align_bytes=64)
+            xs = xp.tile([P, P], U8, name="xs", align_bytes=64)
+            nc.vector.quantize_mx(out=xc[:].bitcast(FP8X4), scales=xs[:], in_=xg[:].rearrange("p d n t -> p (d n t)"))
+            res = []
+            for g in range(2):
+                acc = psa.tile([P, F1], F32, name="acc")
+                nc.tensor.matmul_mx(
+                    out=acc[:],
+                    lhsT=xc[:].bitcast(FP8X4),
+                    lhsT_scale=xs[:],
+                    rhs=w0[:, g, :].bitcast(FP4X4),
+                    rhs_scale=w0s[:, g, :],
+                    start=True,
+                    stop=True,
+                )
+                uv = uvp.tile([P, 4, P], F32, name="uv%d" % g, align_bytes=64)
+                src = acc[:].rearrange("p (k t) -> p t k", t=4)
+                if g == 0:
+                    nc.vector.tensor_tensor(out=uv[:], in0=src, in1=b0[:].rearrange("p (k t) -> p t k", t=4), op=ALU.add)
+                else:
+                    nc.scalar.copy(out=uv[:], in_=src)
+                res.append(uv)
+            return res
+
+        def new_grouped():
+            return gp.tile([P, 8, 8, 16, 4], BF16, name="e1", align_bytes=64)
+
+        def edge_chunk(uv, e1, c):
+            z = psz.tile([P, 4, P], F32, name="z", tag="z")
+            for t in range(4):
+                nc.tensor.matmul(z[:, t, :], lhsT=uv[0][:, t, :], rhs=pi_u[:], is_transpose=True, start=True, stop=False)
+                nc.tensor.matmul(z[:, t, :], lhsT=uv[1][:, t, :], rhs=pi_v2[:, 16 * c : 16 * c + P], is_transpose=True, start=False, stop=True)
+            zs = zp.tile([P, P, 4], F32, name="zs")
+            zv = z[:].rearrange("p t e -> p e t")
+            nc.scalar.mul(out=zs[:], in_=zv, mul=ALPHA)
+            nc.vector.tensor_tensor(
+                out=e1[:, :, c, :, :],
+                in0=zv.rearrange("p (h r) t -> p h r t", h=8),
+                in1=zs[:].rearrange("p (h r) t -> p h r t", h=8),
+                op=ALU.max,
+            )
+
+        def quantize_half(e1, hf):
+            ec = gp.tile([P, 512], U32, name="ec%d" % hf, align_bytes=64)
+            es = gp.tile([P, 512], U8, name="es%d" % hf, align_bytes=64)
+            nc.vector.quantize_mx(
+                out=ec[:].bitcast(FP8X4),
+                scales=es[:],
+                in_=e1[:].rearrange("p h c r t -> p (h c r t)")[:, 2048 * hf : 2048 * (hf + 1)],
+            )
+            return ec, es
+
+        def out_chunk(b, h, codes):
+            ec, es = codes[h // 4]
+            cols = slice(P * (h % 4), P * (h % 4) + P)
+            y = op.tile([P, F2], F32, name="y")
+            for f in range(2):
+                acc = psa.tile([P, F1], F32, name="acc")
+                nc.tensor.matmul_mx(
+                    out=acc[:],
+                    lhsT=ec[:, cols].bitcast(FP8X4),
+                    lhsT_scale=es[:, cols],
+                    rhs=w1[:, 1024 * f : 1024 * (f + 1)].bitcast(FP4X4),
+                    rhs_scale=w1s[:, 512 * f : 512 * (f + 1)],
+                    start=True,
+                    stop=True,
+                )
+                nc.vector.tensor_tensor(out=y[:, 512 * f : 512 * (f + 1)], in0=acc[:], in1=b1[:, 512 * f : 512 * (f + 1)], op=ALU.add)
+            o = op.tile([P, F2], F32, name="o")
+            if 8 * b + h in V_ROUTE:
+                nc.vector.scalar_tensor_tensor(out=o[:], in0=y[:], scalar=ALPHA, in1=y[:], op0=ALU.mult, op1=ALU.max)
+            else:
+                r = op.tile([P, F2], F32, name="r")
+                nc.scalar.activation(out=r[:], in_=y[:], func=ACT.Relu, scale=ALPHA - 1.0)
+                nc.gpsimd.tensor_tensor(out=o[:], in0=y[:], in1=r[:], op=ALU.add)
+            dst = out[b, 4 * h : 4 * h + 4].rearrange("l j f -> j l f")
+            m = 16 * (8 - h)
+            nc.sync.dma_start(out=dst[4 * h : N], in_=o[0:m, :])
+            if h > 0:
+                nc.sync.dma_start(out=dst[0 : 4 * h], in_=o[m:P, :])
+
+        uv = node_products(0)
+        e1 = new_grouped()
+        uv_next = None
+        for c in range(8):
+            edge_chunk(uv, e1, c)
+            if c == 4:
+                uv_next = node_products(1)
+        codes = [quantize_half(e1, 0), quantize_half(e1, 1)]
+        for b in range(B):
+            codes_next = None
+            uv = uv_next
+            if b + 1 < B:
+                e1 = new_grouped()
+            for h in range(8):
+                out_chunk(b, h, codes)
+                if b + 1 < B:
+                    edge_chunk(uv, e1, h)
+                if h == 4 and b + 2 < B:
+                    uv_next = node_products(b + 2)
+            if b + 1 < B:
+                codes = [quantize_half(e1, 0), quantize_half(e1, 1)]

@@ -19,7 +19,8 @@ ACT = mybir.ActivationFunctionType
 
 P = 128
 ALPHA = 0.2
-V_ROUTE = (3, 11, 19, 27)
+CHUNKS = 32
+EDGE_LEAD = 11
 
 
 def tile_graph_gan_pa_w4_kernel(tc, x_bytes, x_scale, fe_w0_words, fe_w0_scales, fe_b0, fe_w1_words, fe_w1_scales, fe_b1, out):
@@ -30,9 +31,13 @@ def tile_graph_gan_pa_w4_kernel(tc, x_bytes, x_scale, fe_w0_words, fe_w0_scales,
         uvp = ctx.enter_context(tc.tile_pool(name="uvp", bufs=2))
         zp = ctx.enter_context(tc.tile_pool(name="zp", bufs=3))
         gp = ctx.enter_context(tc.tile_pool(name="gp", bufs=2))
-        op = ctx.enter_context(tc.tile_pool(name="op", bufs=4))
-        psz = ctx.enter_context(tc.psum_pool(name="psz", bufs=3))
-        psa = ctx.enter_context(tc.psum_pool(name="psa", bufs=5))
+        yp = ctx.enter_context(tc.tile_pool(name="yp", bufs=6))
+        rp = ctx.enter_context(tc.tile_pool(name="rp", bufs=5))
+        op = ctx.enter_context(tc.tile_pool(name="op", bufs=6))
+        lrp = ctx.enter_context(tc.tile_pool(name="lrp", bufs=2))
+        psz = ctx.enter_context(tc.psum_pool(name="psz", bufs=4))
+        psa = ctx.enter_context(tc.psum_pool(name="psa", bufs=4))
+        ctx.enter_context(tc.manual_schedule())
 
         xb = keep.tile([P, D], U8, name="xb", align_bytes=64)
         nc.sync.dma_start(out=xb[:], in_=x_bytes.rearrange("b n k -> (b n) k"))
@@ -65,6 +70,17 @@ def tile_graph_gan_pa_w4_kernel(tc, x_bytes, x_scale, fe_w0_words, fe_w0_scales,
         b1 = keep.tile([P, F2], BF16, name="b1")
         nc.sync.dma_start(out=b1[:], in_=fe_b1.partition_broadcast(P))
 
+        zeros = keep.tile([P, 512], BF16, name="zeros", align_bytes=64)
+        nc.gpsimd.memset(zeros[:], 0.0)
+
+        def keep_busy(n):
+            idle = psa.tile([P, F1], F32, name="acc")
+            for i in range(n):
+                nc.tensor.matmul(idle[:], lhsT=zeros[:, 0:P], rhs=zeros[:], start=True, stop=True)
+
+        keep_busy(5)
+        b1c = keep.tile([P, 8], F32, name="b1c")
+        b1a = keep.tile([P, 8], F32, name="b1a")
         warm = keep.tile([P, 1], F32, name="warm")
         nc.vector.memset(warm[:], 0.0)
         nc.scalar.activation(out=warm[:], in_=warm[:], func=ACT.Relu)
@@ -73,18 +89,6 @@ def tile_graph_gan_pa_w4_kernel(tc, x_bytes, x_scale, fe_w0_words, fe_w0_scales,
         make_identity(nc, identb[:])
         ident = keep.tile([P, P], F32, name="ident")
         make_identity(nc, ident[:])
-        pi_u = keep.tile([P, P], F32, name="pi_u", align_bytes=64)
-        nc.vector.tensor_copy(
-            out=pi_u[:].rearrange("p (h j l) -> p h j l", h=8, j=4),
-            in_=ident[:].rearrange("p (j h l) -> p h j l", h=8, j=4),
-        )
-        pi_v = keep.tile([P, 2, P], F32, name="pi_v", align_bytes=64)
-        for i in range(2):
-            nc.vector.tensor_copy(
-                out=pi_v[:, i, :].rearrange("p (h j l) -> p h j l", h=8, j=4),
-                in_=ident[:].rearrange("p (l h j) -> p h j l", h=8, j=4),
-            )
-        pi_v2 = pi_v[:].rearrange("p i e -> p (i e)")
 
         xw = keep.tile([P, D], BF16, name="xw", align_bytes=64)
         nc.vector.tensor_copy(out=xw[:], in_=xb[:].bitcast(E4M3))
@@ -92,113 +96,262 @@ def tile_graph_gan_pa_w4_kernel(tc, x_bytes, x_scale, fe_w0_words, fe_w0_scales,
         for t in range(4):
             nc.tensor.transpose(xt[:, t, :], xw[:].rearrange("p (k t) -> p t k", t=4)[:, t, :], identb[:])
 
-        def node_products(b):
+        keep_busy(5)
+        nodes = {}
+        edges = {}
+        grouped = {}
+        codes = {}
+        chunk = {}
+        channel = {}
+
+        def node_spread(b):
             xg = xp.tile([P, 4, N, 4], BF16, name="xg", align_bytes=64)
-            nc.vector.tensor_tensor(
-                out=xg[:],
-                in0=xt[:].rearrange("p t m -> p m t")[:, b * N : (b + 1) * N, :].unsqueeze(1).to_broadcast([P, 4, N, 4]),
-                in1=xsc[:].unsqueeze(1).unsqueeze(1).to_broadcast([P, 4, N, 4]),
-                op=ALU.mult,
-            )
+            if b == 0:
+                nc.vector.tensor_tensor(
+                    out=xg[:],
+                    in0=xt_s[:, 0:N, :].unsqueeze(1).to_broadcast([P, 4, N, 4]),
+                    in1=xsc[:].unsqueeze(1).unsqueeze(1).to_broadcast([P, 4, N, 4]),
+                    op=ALU.mult,
+                )
+            else:
+                nc.vector.tensor_copy(out=xg[:], in_=xn[:, b - 1, :, :].unsqueeze(1).to_broadcast([P, 4, N, 4]))
+            nodes[b] = xg
+
+        def node_quantize(b):
             xc = xp.tile([P, P], U32, name="xc", align_bytes=64)
             xs = xp.tile([P, P], U8, name="xs", align_bytes=64)
-            nc.vector.quantize_mx(out=xc[:].bitcast(FP8X4), scales=xs[:], in_=xg[:].rearrange("p d n t -> p (d n t)"))
-            res = []
+            nc.vector.quantize_mx(out=xc[:].bitcast(FP8X4), scales=xs[:], in_=nodes[b][:].rearrange("p d n t -> p (d n t)"))
+            nodes[b] = [xc, xs]
+
+        def node_matmul(b):
+            xc, xs = nodes[b]
             for g in range(2):
                 acc = psa.tile([P, F1], F32, name="acc")
                 nc.tensor.matmul_mx(
-                    out=acc[:],
-                    lhsT=xc[:].bitcast(FP8X4),
-                    lhsT_scale=xs[:],
-                    rhs=w0[:, g, :].bitcast(FP4X4),
-                    rhs_scale=w0s[:, g, :],
-                    start=True,
-                    stop=True,
+                    out=acc[:], lhsT=xc[:].bitcast(FP8X4), lhsT_scale=xs[:], rhs=w0[:, g, :].bitcast(FP4X4), rhs_scale=w0s[:, g, :], start=True, stop=True
                 )
-                uv = uvp.tile([P, 4, P], F32, name="uv%d" % g, align_bytes=64)
-                src = acc[:].rearrange("p (k t) -> p t k", t=4)
-                if g == 0:
-                    nc.vector.tensor_tensor(out=uv[:], in0=src, in1=b0[:].rearrange("p (k t) -> p t k", t=4), op=ALU.add)
-                else:
-                    nc.scalar.copy(out=uv[:], in_=src)
-                res.append(uv)
-            return res
+                nodes[b].append(acc)
 
-        def new_grouped():
-            return gp.tile([P, 8, 8, 16, 4], BF16, name="e1", align_bytes=64)
+        def node_evacuate(b):
+            u = uvp.tile([P, 4, P], F32, name="u", align_bytes=64)
+            nc.vector.tensor_tensor(
+                out=u[:], in0=nodes[b][2][:].rearrange("p (k t) -> p t k", t=4), in1=b0[:].rearrange("p (k t) -> p t k", t=4), op=ALU.add
+            )
+            v = uvp.tile([P, 4, P], F32, name="v", align_bytes=64)
+            nc.scalar.copy(out=v[:], in_=nodes[b][3][:].rearrange("p (k t) -> p t k", t=4))
+            nodes[b] += [u, v]
 
-        def edge_chunk(uv, e1, c):
+        def edge_sum(k):
+            u, v = nodes[k // 8][4:6]
+            c = k % 8
             z = psz.tile([P, 4, P], F32, name="z", tag="z")
             for t in range(4):
-                nc.tensor.matmul(z[:, t, :], lhsT=uv[0][:, t, :], rhs=pi_u[:], is_transpose=True, start=True, stop=False)
-                nc.tensor.matmul(z[:, t, :], lhsT=uv[1][:, t, :], rhs=pi_v2[:, 16 * c : 16 * c + P], is_transpose=True, start=False, stop=True)
+                nc.tensor.matmul(z[:, t, :], lhsT=u[:, t, :], rhs=pi_u[:], is_transpose=True, start=True, stop=False)
+                nc.tensor.matmul(z[:, t, :], lhsT=v[:, t, :], rhs=pi_v2[:, 16 * c : 16 * c + P], is_transpose=True, start=False, stop=True)
+            edges[k] = z
+
+        def edge_scale(k):
             zs = zp.tile([P, P, 4], F32, name="zs")
-            zv = z[:].rearrange("p t e -> p e t")
-            nc.scalar.mul(out=zs[:], in_=zv, mul=ALPHA)
+            nc.scalar.mul(out=zs[:], in_=edges[k][:].rearrange("p t e -> p e t"), mul=ALPHA)
+            edges[k] = (edges[k], zs)
+
+        def edge_max(k):
+            b, c = divmod(k, 8)
+            if c == 0:
+                grouped[b] = gp.tile([P, 8, 8, 16, 4], BF16, name="e1", align_bytes=64)
+            z, zs = edges.pop(k)
             nc.vector.tensor_tensor(
-                out=e1[:, :, c, :, :],
-                in0=zv.rearrange("p (h r) t -> p h r t", h=8),
+                out=grouped[b][:, :, c, :, :],
+                in0=z[:].rearrange("p t (h r) -> p h r t", h=8),
                 in1=zs[:].rearrange("p (h r) t -> p h r t", h=8),
                 op=ALU.max,
             )
 
-        def quantize_half(e1, hf):
-            ec = gp.tile([P, 512], U32, name="ec%d" % hf, align_bytes=64)
-            es = gp.tile([P, 512], U8, name="es%d" % hf, align_bytes=64)
-            nc.vector.quantize_mx(
-                out=ec[:].bitcast(FP8X4),
-                scales=es[:],
-                in_=e1[:].rearrange("p h c r t -> p (h c r t)")[:, 2048 * hf : 2048 * (hf + 1)],
-            )
-            return ec, es
+        def edge_quantize(k):
+            b, c = divmod(k, 8)
+            if c < 7:
+                return
+            e1 = grouped[b][:].rearrange("p h c r t -> p (h c r t)")
+            for hf in range(2):
+                ec = gp.tile([P, 512], U32, name="ec%d" % hf, align_bytes=64)
+                es = gp.tile([P, 512], U8, name="es%d" % hf, align_bytes=64)
+                nc.vector.quantize_mx(out=ec[:].bitcast(FP8X4), scales=es[:], in_=e1[:, 2048 * hf : 2048 * (hf + 1)])
+                codes[2 * b + hf] = (ec, es)
 
-        def out_chunk(b, h, codes):
-            ec, es = codes[h // 4]
-            cols = slice(P * (h % 4), P * (h % 4) + P)
-            y = op.tile([P, F2], F32, name="y")
-            for f in range(2):
+        def widths(s):
+            return (768, 0) if s < 24 else (512, 0)
+
+        def groups(s):
+            wg, wf = widths(s)
+            return list(range((wg + wf) // P, 8))
+
+        def out_matmul(s):
+            ec, es = codes[s // 4]
+            cols = slice(P * (s % 4), P * (s % 4) + P)
+            wg, wf = widths(s)
+            chunk[s] = {}
+            for f0 in range(0, wg + wf, 512):
+                n = min(512, wg + wf - f0)
+                acc = psa.tile([P, F1], F32, name="acc")
+                for again in range(2 if f0 == 0 and s % 2 == 0 else 1):
+                    nc.tensor.matmul_mx(
+                        out=acc[:, 0:n],
+                        lhsT=ec[:, cols].bitcast(FP8X4),
+                        lhsT_scale=es[:, cols],
+                        rhs=w1[:, 2 * f0 : 2 * (f0 + n)].bitcast(FP4X4),
+                        rhs_scale=w1s[:, f0 : f0 + n],
+                        start=True,
+                        stop=True,
+                    )
+                chunk[s][f0] = (acc, n)
+
+        def out_add(s, f0):
+            if f0 in chunk[s]:
+                acc, n = chunk[s][f0]
+                nc.vector.tensor_tensor(out=chunk[s]["y"][:, f0 : f0 + n], in0=acc[:, 0:n], in1=b1[:, f0 : f0 + n], op=ALU.add)
+
+        def out_add_first(s):
+            chunk[s]["y"] = yp.tile([P, F2], F32, name="y")
+            out_add(s, 0)
+
+        def out_add_second(s):
+            out_add(s, 512)
+
+        def out_relu(s):
+            wg, wf = widths(s)
+            r = rp.tile([P, F2], F32, name="r")
+            nc.scalar.activation(out=r[:, 0:wg], in_=chunk[s]["y"][:, 0:wg], func=ACT.Relu, scale=ALPHA - 1.0)
+            chunk[s]["r"] = r
+
+        def out_tile(s):
+            if "o" not in chunk[s]:
+                chunk[s]["o"] = op.tile([P, F2], F32, name="o")
+            return chunk[s]["o"]
+
+        def out_gpsimd(s):
+            wg, wf = widths(s)
+            o = out_tile(s)
+            nc.gpsimd.tensor_tensor(out=o[:, 0:wg], in0=chunk[s]["y"][:, 0:wg], in1=chunk[s]["r"][:, 0:wg], op=ALU.add)
+
+        def out_vector(s):
+            wg, wf = widths(s)
+            if wf:
+                o = out_tile(s)
+                y = chunk[s]["y"][:, wg : wg + wf]
+                nc.vector.scalar_tensor_tensor(out=o[:, wg : wg + wf], in0=y, scalar=ALPHA, in1=y, op0=ALU.mult, op1=ALU.max)
+
+        def channel_work(s):
+            q, i = divmod(s, 4)
+            return [(q, g) for n, g in enumerate(groups(s)) if n % 2 == i]
+
+        def channel_matmul(s):
+            for q, g in channel_work(s):
+                ec, es = codes[q]
                 acc = psa.tile([P, F1], F32, name="acc")
                 nc.tensor.matmul_mx(
                     out=acc[:],
-                    lhsT=ec[:, cols].bitcast(FP8X4),
-                    lhsT_scale=es[:, cols],
-                    rhs=w1[:, 1024 * f : 1024 * (f + 1)].bitcast(FP4X4),
-                    rhs_scale=w1s[:, 512 * f : 512 * (f + 1)],
+                    lhsT=w1[:, 256 * g : 256 * (g + 1)].bitcast(FP4X4),
+                    lhsT_scale=w1s[:, P * g : P * (g + 1)],
+                    rhs=ec[:].bitcast(FP8X4),
+                    rhs_scale=es[:],
                     start=True,
                     stop=True,
                 )
-                nc.vector.tensor_tensor(out=y[:, 512 * f : 512 * (f + 1)], in0=acc[:], in1=b1[:, 512 * f : 512 * (f + 1)], op=ALU.add)
-            o = op.tile([P, F2], F32, name="o")
-            if 8 * b + h in V_ROUTE:
-                nc.vector.scalar_tensor_tensor(out=o[:], in0=y[:], scalar=ALPHA, in1=y[:], op0=ALU.mult, op1=ALU.max)
+                channel[q, g] = acc
+
+        def channel_scale(s):
+            for q, g in channel_work(s):
+                ys = zp.tile([P, 512], F32, name="ys")
+                nc.scalar.activation(out=ys[:], in_=channel[q, g][:], func=ACT.Identity, scale=ALPHA, bias=b1a[:, g : g + 1])
+                channel[q, g] = (channel[q, g], ys)
+
+        def channel_max(s):
+            for q, g in channel_work(s):
+                acc, ys = channel[q, g]
+                lr = lrp.tile([P, 512], F32, name="lr%d" % (g % 4))
+                nc.vector.scalar_tensor_tensor(out=lr[:], in0=acc[:], scalar=b1c[:, g : g + 1], in1=ys[:], op0=ALU.add, op1=ALU.max)
+                channel[q, g] = lr
+
+        def out_transpose(s):
+            cols = slice(P * (s % 4), P * (s % 4) + P)
+            tr = psz.tile([P, 4, P], F32, name="tr", tag="z")
+            for i, g in enumerate(groups(s)):
+                nc.tensor.transpose(tr[:, i, :], channel[s // 4, g][:, cols], ident[:])
+            chunk[s]["tr"] = tr
+
+        def out_copy(s):
+            gs = groups(s)
+            o = out_tile(s)
+            tr = chunk[s]["tr"][:, 0 : len(gs), :].rearrange("p i e -> p (i e)")
+            if s % 4 == 0:
+                nc.vector.tensor_copy(out=o[:, P * gs[0] : F2], in_=tr)
             else:
-                r = op.tile([P, F2], F32, name="r")
-                nc.scalar.activation(out=r[:], in_=y[:], func=ACT.Relu, scale=ALPHA - 1.0)
-                nc.gpsimd.tensor_tensor(out=o[:], in0=y[:], in1=r[:], op=ALU.add)
+                nc.scalar.copy(out=o[:, P * gs[0] : F2], in_=tr)
+
+        def out_store(s):
+            o = chunk[s]["o"]
+            b, h = divmod(s, 8)
             dst = out[b, 4 * h : 4 * h + 4].rearrange("l j f -> j l f")
             m = 16 * (8 - h)
             nc.sync.dma_start(out=dst[4 * h : N], in_=o[0:m, :])
             if h > 0:
                 nc.sync.dma_start(out=dst[0 : 4 * h], in_=o[m:P, :])
 
-        uv = node_products(0)
-        e1 = new_grouped()
-        uv_next = None
-        for c in range(8):
-            edge_chunk(uv, e1, c)
-            if c == 4:
-                uv_next = node_products(1)
-        codes = [quantize_half(e1, 0), quantize_half(e1, 1)]
-        for b in range(B):
-            codes_next = None
-            uv = uv_next
-            if b + 1 < B:
-                e1 = new_grouped()
-            for h in range(8):
-                out_chunk(b, h, codes)
-                if b + 1 < B:
-                    edge_chunk(uv, e1, h)
-                if h == 4 and b + 2 < B:
-                    uv_next = node_products(b + 2)
-            if b + 1 < B:
-                codes = [quantize_half(e1, 0), quantize_half(e1, 1)]
+        xt_s = xt[:].rearrange("p t m -> p m t")
+        node_spread(0)
+        xn = keep.tile([P, 3, N, 4], BF16, name="xn", align_bytes=64)
+        nc.vector.tensor_tensor(
+            out=xn[:].rearrange("p b n t -> p (b n) t"), in0=xt_s[:, N : 4 * N, :], in1=xsc[:].unsqueeze(1).to_broadcast([P, 3 * N, 4]), op=ALU.mult
+        )
+        node_quantize(0)
+        pi_u = keep.tile([P, P], F32, name="pi_u", align_bytes=64)
+        nc.vector.tensor_copy(
+            out=pi_u[:].rearrange("p (h j l) -> p h j l", h=8, j=4), in_=ident[:].rearrange("p (j h l) -> p h j l", h=8, j=4)
+        )
+        pi_v = keep.tile([P, 2, P], F32, name="pi_v", align_bytes=64)
+        for i in range(2):
+            nc.vector.tensor_copy(
+                out=pi_v[:, i, :].rearrange("p (h j l) -> p h j l", h=8, j=4), in_=ident[:].rearrange("p (l h j) -> p h j l", h=8, j=4)
+            )
+        pi_v2 = pi_v[:].rearrange("p i e -> p (i e)")
+        node_matmul(0)
+        keep_busy(2)
+        node_evacuate(0)
+        stages = (
+            (out_add_first, 2),
+            (out_matmul, 1),
+            (channel_matmul, 0),
+            (out_relu, 3),
+            (out_transpose, 3),
+            (edge_max, -9),
+            (edge_scale, -10),
+            (channel_scale, 0),
+            (out_gpsimd, 4),
+            (out_add_second, 2),
+            (out_store, 5),
+            (channel_max, 1),
+            (edge_quantize, -9),
+            (out_vector, 2),
+            (edge_sum, -11),
+            (out_copy, 4),
+        )
+        for s in range(-EDGE_LEAD, CHUNKS + 6):
+            if s == -3:
+                bt = psa.tile([P, 8, P], BF16, name="bt", tag="acc")
+                for g in range(8):
+                    nc.tensor.transpose(bt[:, g, :], b1[:, P * g : P * (g + 1)], identb[:])
+                nc.vector.tensor_copy(out=b1c[:], in_=bt[:, :, 0])
+                nc.vector.tensor_scalar(out=b1a[:], in0=bt[:, :, 0], scalar1=ALPHA, scalar2=None, op0=ALU.mult)
+            for stage, lag in stages:
+                if 0 <= s - lag < CHUNKS:
+                    stage(s - lag)
+            for b in range(1, B):
+                first = 8 * b - EDGE_LEAD
+                if s == first - 5:
+                    node_spread(b)
+                if s == first - 4:
+                    node_quantize(b)
+                if s == first - 3:
+                    node_matmul(b)
+                if s == first - 2:
+                    node_evacuate(b)

@@ -31,9 +31,9 @@ def tile_graph_gan_pa_w4_kernel(tc, x_bytes, x_scale, fe_w0_words, fe_w0_scales,
         uvp = ctx.enter_context(tc.tile_pool(name="uvp", bufs=2))
         zp = ctx.enter_context(tc.tile_pool(name="zp", bufs=3))
         gp = ctx.enter_context(tc.tile_pool(name="gp", bufs=2))
-        yp = ctx.enter_context(tc.tile_pool(name="yp", bufs=6))
-        rp = ctx.enter_context(tc.tile_pool(name="rp", bufs=5))
-        op = ctx.enter_context(tc.tile_pool(name="op", bufs=6))
+        yp = ctx.enter_context(tc.tile_pool(name="yp", bufs=7))
+        rp = ctx.enter_context(tc.tile_pool(name="rp", bufs=8))
+        op = ctx.enter_context(tc.tile_pool(name="op", bufs=5))
         lrp = ctx.enter_context(tc.tile_pool(name="lrp", bufs=2))
         psz = ctx.enter_context(tc.psum_pool(name="psz", bufs=4))
         psa = ctx.enter_context(tc.psum_pool(name="psa", bufs=4))
@@ -43,42 +43,47 @@ def tile_graph_gan_pa_w4_kernel(tc, x_bytes, x_scale, fe_w0_words, fe_w0_scales,
         nc.sync.dma_start(out=xb[:], in_=x_bytes.rearrange("b n k -> (b n) k"))
         xsc = keep.tile([P, 4], F32, name="xsc")
         nc.sync.dma_start(out=xsc[:], in_=x_scale.rearrange("o q (p t) -> p (o q t)", t=4))
-        w0 = keep.tile([P, 2, 2 * F1], U8, name="w0", align_bytes=64)
-        nc.sync.dma_start(
-            out=w0[:].rearrange("p g n -> p (g n)").bitcast(I32).rearrange("p (g n) -> p g n", g=2),
-            in_=fe_w0_words.bitcast(I32).rearrange("g p n -> p g n"),
-        )
         w0s = keep.tile([P, 2, F1], U8, name="w0s", align_bytes=64)
         w0s_i = w0s[:].rearrange("p g n -> p (g n)").bitcast(I32)
         nc.vector.memset(w0s_i, 0)
         w1s = keep.tile([P, F2], U8, name="w1s", align_bytes=64)
         nc.vector.memset(w1s[:].bitcast(I32), 0)
+        brow = keep.tile([P, F1 + F2], BF16, name="brow", align_bytes=64)
+        nc.gpsimd.memset(brow[:].bitcast(I32), 0)
+        first_row = keep.tile([P, P], BF16, name="first_row", align_bytes=64)
+        nc.vector.memset(first_row[:], 0.0)
+        nc.vector.memset(first_row[0:1, :], 1.0)
+        nc.scalar.dma_start(out=brow[0:1, 0:F1], in_=fe_b0.rearrange("(o n) -> o n", o=1))
+        nc.scalar.dma_start(out=brow[0:1, F1 : F1 + F2], in_=fe_b1.rearrange("(o n) -> o n", o=1))
         for q in range(4):
             nc.sync.dma_start(
                 out=w0s_i.rearrange("p (g n) -> p g n", g=2)[32 * q : 32 * q + 4],
                 in_=fe_w0_scales.bitcast(I32)[:, 4 * q : 4 * q + 4, :].rearrange("g r n -> r g n"),
             )
-        b0 = keep.tile([P, F1], BF16, name="b0")
-        nc.sync.dma_start(out=b0[:], in_=fe_b0.partition_broadcast(P))
-        w1 = keep.tile([P, 2 * F2], U8, name="w1", align_bytes=64)
-        nc.sync.dma_start(out=w1[:].bitcast(I32), in_=fe_w1_words.bitcast(I32)[0])
+        w0 = keep.tile([P, 2, 2 * F1], U8, name="w0", align_bytes=64)
+        nc.sync.dma_start(
+            out=w0[:].rearrange("p g n -> p (g n)").bitcast(I32).rearrange("p (g n) -> p g n", g=2),
+            in_=fe_w0_words.bitcast(I32).rearrange("g p n -> p g n"),
+        )
         for q in range(4):
             nc.sync.dma_start(
                 out=w1s[:].bitcast(I32)[32 * q : 32 * q + 4],
                 in_=fe_w1_scales.bitcast(I32)[0, 4 * q : 4 * q + 4, :],
             )
-        b1 = keep.tile([P, F2], BF16, name="b1")
-        nc.sync.dma_start(out=b1[:], in_=fe_b1.partition_broadcast(P))
+        w1 = keep.tile([P, 2 * F2], U8, name="w1", align_bytes=64)
+        nc.sync.dma_start(out=w1[:].bitcast(I32), in_=fe_w1_words.bitcast(I32)[0])
+        b0 = keep.tile([P, 4, P], BF16, name="b0", align_bytes=64)
+        b1 = keep.tile([P, F2], BF16, name="b1", align_bytes=64)
 
         zeros = keep.tile([P, 512], BF16, name="zeros", align_bytes=64)
-        nc.gpsimd.memset(zeros[:], 0.0)
+        nc.vector.memset(zeros[:], 0.0)
 
         def keep_busy(n):
             idle = psa.tile([P, F1], F32, name="acc")
             for i in range(n):
                 nc.tensor.matmul(idle[:], lhsT=zeros[:, 0:P], rhs=zeros[:], start=True, stop=True)
 
-        keep_busy(5)
+        keep_busy(4)
         b1c = keep.tile([P, 8], F32, name="b1c")
         b1a = keep.tile([P, 8], F32, name="b1a")
         warm = keep.tile([P, 1], F32, name="warm")
@@ -96,7 +101,14 @@ def tile_graph_gan_pa_w4_kernel(tc, x_bytes, x_scale, fe_w0_words, fe_w0_scales,
         for t in range(4):
             nc.tensor.transpose(xt[:, t, :], xw[:].rearrange("p (k t) -> p t k", t=4)[:, t, :], identb[:])
 
-        keep_busy(5)
+        for n0 in range(0, F1 + F2, 512):
+            acc = psa.tile([P, F1], F32, name="acc")
+            nc.tensor.matmul(acc[:], lhsT=first_row[:], rhs=brow[:, n0 : n0 + 512], start=True, stop=True)
+            if n0 == 0:
+                nc.scalar.copy(out=b0[:], in_=acc[:].rearrange("p (k t) -> p t k", t=4))
+            else:
+                nc.scalar.copy(out=b1[:, n0 - F1 : n0 - F1 + 512], in_=acc[:])
+        keep_busy(2)
         nodes = {}
         edges = {}
         grouped = {}
@@ -135,7 +147,7 @@ def tile_graph_gan_pa_w4_kernel(tc, x_bytes, x_scale, fe_w0_words, fe_w0_scales,
         def node_evacuate(b):
             u = uvp.tile([P, 4, P], F32, name="u", align_bytes=64)
             nc.vector.tensor_tensor(
-                out=u[:], in0=nodes[b][2][:].rearrange("p (k t) -> p t k", t=4), in1=b0[:].rearrange("p (k t) -> p t k", t=4), op=ALU.add
+                out=u[:], in0=nodes[b][2][:].rearrange("p (k t) -> p t k", t=4), in1=b0[:], op=ALU.add
             )
             v = uvp.tile([P, 4, P], F32, name="v", align_bytes=64)
             nc.scalar.copy(out=v[:], in_=nodes[b][3][:].rearrange("p (k t) -> p t k", t=4))
@@ -147,7 +159,7 @@ def tile_graph_gan_pa_w4_kernel(tc, x_bytes, x_scale, fe_w0_words, fe_w0_scales,
             z = psz.tile([P, 4, P], F32, name="z", tag="z")
             for t in range(4):
                 nc.tensor.matmul(z[:, t, :], lhsT=u[:, t, :], rhs=pi_u[:], is_transpose=True, start=True, stop=False)
-                nc.tensor.matmul(z[:, t, :], lhsT=v[:, t, :], rhs=pi_v2[:, 16 * c : 16 * c + P], is_transpose=True, start=False, stop=True)
+                nc.tensor.matmul(z[:, t, :], lhsT=v[:, t, :], rhs=pi_v[:, c, :, :].rearrange("p h e -> p (h e)"), is_transpose=True, start=False, stop=True)
             edges[k] = z
 
         def edge_scale(k):
@@ -158,20 +170,31 @@ def tile_graph_gan_pa_w4_kernel(tc, x_bytes, x_scale, fe_w0_words, fe_w0_scales,
         def edge_max(k):
             b, c = divmod(k, 8)
             if c == 0:
-                grouped[b] = gp.tile([P, 8, 8, 16, 4], BF16, name="e1", align_bytes=64)
+                grouped[b] = gp.tile([P, 76, 64], BF16, name="e1", align_bytes=64)
             z, zs = edges.pop(k)
-            nc.vector.tensor_tensor(
-                out=grouped[b][:, :, c, :, :],
-                in0=z[:].rearrange("p t (h r) -> p h r t", h=8),
-                in1=zs[:].rearrange("p (h r) t -> p h r t", h=8),
-                op=ALU.max,
-            )
+            z = z[:].rearrange("p t (h r) -> p h r t", h=8)
+            zs = zs[:].rearrange("p (h r) t -> p h r t", h=8)
+            step = [(7 if c >> i & 1 else 9) << i for i in range(3)]
+            if step[1] == 2 * step[0]:
+                runs = [(0, c, 2, step[2], 4, step[0])]
+            elif step[2] == 2 * step[1]:
+                runs = [(0, c, 4, step[1], 2, step[0])]
+            else:
+                runs = [(4 * h, c + h * step[2], 2, step[1], 2, step[0]) for h in range(2)]
+            for h, first, na, sa, nb, sb in runs:
+                dst = grouped[b][:, first : first + na * sa, :].rearrange("p (a x) (r t) -> p a x r t", a=na, t=4)
+                nc.vector.tensor_tensor(
+                    out=dst[:, :, 0 : (nb - 1) * sb + 1 : sb, :, :],
+                    in0=z[:, h : h + na * nb, :, :].rearrange("p (a x) r t -> p a x r t", a=na),
+                    in1=zs[:, h : h + na * nb, :, :].rearrange("p (a x) r t -> p a x r t", a=na),
+                    op=ALU.max,
+                )
 
         def edge_quantize(k):
             b, c = divmod(k, 8)
             if c < 7:
                 return
-            e1 = grouped[b][:].rearrange("p h c r t -> p (h c r t)")
+            e1 = grouped[b][:].rearrange("p i e -> p (i e)")
             for hf in range(2):
                 ec = gp.tile([P, 512], U32, name="ec%d" % hf, align_bytes=64)
                 es = gp.tile([P, 512], U8, name="es%d" % hf, align_bytes=64)
@@ -193,16 +216,15 @@ def tile_graph_gan_pa_w4_kernel(tc, x_bytes, x_scale, fe_w0_words, fe_w0_scales,
             for f0 in range(0, wg + wf, 512):
                 n = min(512, wg + wf - f0)
                 acc = psa.tile([P, F1], F32, name="acc")
-                for again in range(2 if f0 == 0 and s % 2 == 0 else 1):
-                    nc.tensor.matmul_mx(
-                        out=acc[:, 0:n],
-                        lhsT=ec[:, cols].bitcast(FP8X4),
-                        lhsT_scale=es[:, cols],
-                        rhs=w1[:, 2 * f0 : 2 * (f0 + n)].bitcast(FP4X4),
-                        rhs_scale=w1s[:, f0 : f0 + n],
-                        start=True,
-                        stop=True,
-                    )
+                nc.tensor.matmul_mx(
+                    out=acc[:, 0:n],
+                    lhsT=ec[:, cols].bitcast(FP8X4),
+                    lhsT_scale=es[:, cols],
+                    rhs=w1[:, 2 * f0 : 2 * (f0 + n)].bitcast(FP4X4),
+                    rhs_scale=w1s[:, f0 : f0 + n],
+                    start=True,
+                    stop=True,
+                )
                 chunk[s][f0] = (acc, n)
 
         def out_add(s, f0):
@@ -292,10 +314,7 @@ def tile_graph_gan_pa_w4_kernel(tc, x_bytes, x_scale, fe_w0_words, fe_w0_scales,
             o = chunk[s]["o"]
             b, h = divmod(s, 8)
             dst = out[b, 4 * h : 4 * h + 4].rearrange("l j f -> j l f")
-            m = 16 * (8 - h)
-            nc.sync.dma_start(out=dst[4 * h : N], in_=o[0:m, :])
-            if h > 0:
-                nc.sync.dma_start(out=dst[0 : 4 * h], in_=o[m:P, :])
+            nc.sync.dma_start(out=dst, in_=o[:])
 
         xt_s = xt[:].rearrange("p t m -> p m t")
         node_spread(0)
@@ -308,32 +327,37 @@ def tile_graph_gan_pa_w4_kernel(tc, x_bytes, x_scale, fe_w0_words, fe_w0_scales,
         nc.vector.tensor_copy(
             out=pi_u[:].rearrange("p (h j l) -> p h j l", h=8, j=4), in_=ident[:].rearrange("p (j h l) -> p h j l", h=8, j=4)
         )
-        pi_v = keep.tile([P, 2, P], F32, name="pi_v", align_bytes=64)
-        for i in range(2):
-            nc.vector.tensor_copy(
-                out=pi_v[:, i, :].rearrange("p (h j l) -> p h j l", h=8, j=4), in_=ident[:].rearrange("p (l h j) -> p h j l", h=8, j=4)
-            )
-        pi_v2 = pi_v[:].rearrange("p i e -> p (i e)")
+        pi_v = keep.tile([P, 8, 8, 16], F32, name="pi_v", align_bytes=64)
+        nc.vector.tensor_copy(
+            out=pi_v[:, 0, :, :].rearrange("p h (j l) -> p h j l", j=4), in_=ident[:].rearrange("p (l h j) -> p h j l", h=8, j=4)
+        )
+        for w in (1, 2, 4):
+            for half in range(2):
+                eng = nc.gpsimd if w == 4 else nc.vector
+                eng.tensor_copy(
+                    out=pi_v[:, w : 2 * w, :, :].rearrange("p c (a x b) e -> p c a x (b e)", x=2, b=w)[:, :, :, half, :],
+                    in_=pi_v[:, 0:w, :, :].rearrange("p c (a x b) e -> p c a x (b e)", x=2, b=w)[:, :, :, 1 - half, :],
+                )
         node_matmul(0)
-        keep_busy(2)
+        keep_busy(1)
         node_evacuate(0)
         stages = (
-            (out_add_first, 2),
-            (out_matmul, 1),
+            (out_vector, 3),
+            (channel_max, 2),
+            (channel_scale, 1),
+            (out_matmul, 0),
             (channel_matmul, 0),
-            (out_relu, 3),
-            (out_transpose, 3),
-            (edge_max, -9),
-            (edge_scale, -10),
-            (channel_scale, 0),
-            (out_gpsimd, 4),
-            (out_add_second, 2),
-            (out_store, 5),
-            (channel_max, 1),
-            (edge_quantize, -9),
-            (out_vector, 2),
-            (edge_sum, -11),
+            (edge_quantize, -8),
+            (out_add_first, 1),
             (out_copy, 4),
+            (out_gpsimd, 4),
+            (edge_max, -9),
+            (out_relu, 2),
+            (out_store, 4),
+            (out_transpose, 3),
+            (out_add_second, 1),
+            (edge_scale, -10),
+            (edge_sum, -11),
         )
         for s in range(-EDGE_LEAD, CHUNKS + 6):
             if s == -3:

@@ -27,7 +27,7 @@ def tile_graph_gan_pa_w4_kernel(tc, x_bytes, x_scale, fe_w0_words, fe_w0_scales,
     nc = tc.nc
     with ExitStack() as ctx:
         keep = ctx.enter_context(tc.tile_pool(name="keep", bufs=1))
-        xp = ctx.enter_context(tc.tile_pool(name="xp", bufs=2))
+        xp = ctx.enter_context(tc.tile_pool(name="xp", bufs=4))
         uvp = ctx.enter_context(tc.tile_pool(name="uvp", bufs=2))
         zp = ctx.enter_context(tc.tile_pool(name="zp", bufs=3))
         gp = ctx.enter_context(tc.tile_pool(name="gp", bufs=2))
@@ -101,14 +101,10 @@ def tile_graph_gan_pa_w4_kernel(tc, x_bytes, x_scale, fe_w0_words, fe_w0_scales,
         for t in range(4):
             nc.tensor.transpose(xt[:, t, :], xw[:].rearrange("p (k t) -> p t k", t=4)[:, t, :], identb[:])
 
-        for n0 in range(0, F1 + F2, 512):
-            acc = psa.tile([P, F1], F32, name="acc")
-            nc.tensor.matmul(acc[:], lhsT=first_row[:], rhs=brow[:, n0 : n0 + 512], start=True, stop=True)
-            if n0 == 0:
-                nc.scalar.copy(out=b0[:], in_=acc[:].rearrange("p (k t) -> p t k", t=4))
-            else:
-                nc.scalar.copy(out=b1[:, n0 - F1 : n0 - F1 + 512], in_=acc[:])
-        keep_busy(2)
+        acc = psa.tile([P, F1], F32, name="acc")
+        nc.tensor.matmul(acc[:], lhsT=first_row[:], rhs=brow[:, 0:F1], start=True, stop=True)
+        nc.scalar.copy(out=b0[:], in_=acc[:].rearrange("p (k t) -> p t k", t=4))
+        keep_busy(4)
         nodes = {}
         edges = {}
         grouped = {}
@@ -146,9 +142,12 @@ def tile_graph_gan_pa_w4_kernel(tc, x_bytes, x_scale, fe_w0_words, fe_w0_scales,
 
         def node_evacuate(b):
             u = uvp.tile([P, 4, P], F32, name="u", align_bytes=64)
-            nc.vector.tensor_tensor(
-                out=u[:], in0=nodes[b][2][:].rearrange("p (k t) -> p t k", t=4), in1=b0[:], op=ALU.add
-            )
+            if b in (9,):
+                ua = uvp.tile([P, 4, P], F32, name="ua", align_bytes=64)
+                nc.scalar.copy(out=ua[:], in_=nodes[b][2][:].rearrange("p (k t) -> p t k", t=4))
+                nc.gpsimd.tensor_tensor(out=u[:], in0=ua[:], in1=b0[:], op=ALU.add)
+            else:
+                nc.vector.tensor_tensor(out=u[:], in0=nodes[b][2][:].rearrange("p (k t) -> p t k", t=4), in1=b0[:], op=ALU.add)
             v = uvp.tile([P, 4, P], F32, name="v", align_bytes=64)
             nc.scalar.copy(out=v[:], in_=nodes[b][3][:].rearrange("p (k t) -> p t k", t=4))
             nodes[b] += [u, v]
@@ -202,7 +201,11 @@ def tile_graph_gan_pa_w4_kernel(tc, x_bytes, x_scale, fe_w0_words, fe_w0_scales,
                 codes[2 * b + hf] = (ec, es)
 
         def widths(s):
-            return (768, 0) if s < 24 else (512, 0)
+            if s < 24:
+                return 768, 0
+            if s < 31:
+                return 512, 0
+            return 256, 256
 
         def groups(s):
             wg, wf = widths(s)
@@ -305,7 +308,7 @@ def tile_graph_gan_pa_w4_kernel(tc, x_bytes, x_scale, fe_w0_words, fe_w0_scales,
             gs = groups(s)
             o = out_tile(s)
             tr = chunk[s]["tr"][:, 0 : len(gs), :].rearrange("p i e -> p (i e)")
-            if s % 4 == 0:
+            if s % 4 == 1:
                 nc.vector.tensor_copy(out=o[:, P * gs[0] : F2], in_=tr)
             else:
                 nc.scalar.copy(out=o[:, P * gs[0] : F2], in_=tr)
@@ -314,7 +317,10 @@ def tile_graph_gan_pa_w4_kernel(tc, x_bytes, x_scale, fe_w0_words, fe_w0_scales,
             o = chunk[s]["o"]
             b, h = divmod(s, 8)
             dst = out[b, 4 * h : 4 * h + 4].rearrange("l j f -> j l f")
-            nc.sync.dma_start(out=dst, in_=o[:])
+            wg = widths(s)[0] if s == CHUNKS - 1 else 0
+            nc.sync.dma_start(out=dst[:, :, wg:F2], in_=o[:, wg:F2])
+            if wg:
+                nc.sync.dma_start(out=dst[:, :, 0:wg], in_=o[:, 0:wg])
 
         xt_s = xt[:].rearrange("p t m -> p m t")
         node_spread(0)
@@ -323,14 +329,19 @@ def tile_graph_gan_pa_w4_kernel(tc, x_bytes, x_scale, fe_w0_words, fe_w0_scales,
             out=xn[:].rearrange("p b n t -> p (b n) t"), in0=xt_s[:, N : 4 * N, :], in1=xsc[:].unsqueeze(1).to_broadcast([P, 3 * N, 4]), op=ALU.mult
         )
         node_quantize(0)
+        node_spread(1)
         pi_u = keep.tile([P, P], F32, name="pi_u", align_bytes=64)
         nc.vector.tensor_copy(
             out=pi_u[:].rearrange("p (h j l) -> p h j l", h=8, j=4), in_=ident[:].rearrange("p (j h l) -> p h j l", h=8, j=4)
         )
+        node_quantize(1)
         pi_v = keep.tile([P, 8, 8, 16], F32, name="pi_v", align_bytes=64)
         nc.vector.tensor_copy(
             out=pi_v[:, 0, :, :].rearrange("p h (j l) -> p h j l", j=4), in_=ident[:].rearrange("p (l h j) -> p h j l", h=8, j=4)
         )
+        node_matmul(0)
+        node_matmul(1)
+        node_evacuate(0)
         for w in (1, 2, 4):
             for half in range(2):
                 eng = nc.gpsimd if w == 4 else nc.vector
@@ -338,9 +349,11 @@ def tile_graph_gan_pa_w4_kernel(tc, x_bytes, x_scale, fe_w0_words, fe_w0_scales,
                     out=pi_v[:, w : 2 * w, :, :].rearrange("p c (a x b) e -> p c a x (b e)", x=2, b=w)[:, :, :, half, :],
                     in_=pi_v[:, 0:w, :, :].rearrange("p c (a x b) e -> p c a x (b e)", x=2, b=w)[:, :, :, 1 - half, :],
                 )
-        node_matmul(0)
-        keep_busy(1)
-        node_evacuate(0)
+        node_evacuate(1)
+        node_spread(2)
+        node_spread(3)
+        node_quantize(2)
+        node_quantize(3)
         stages = (
             (out_vector, 3),
             (channel_max, 2),
@@ -360,6 +373,11 @@ def tile_graph_gan_pa_w4_kernel(tc, x_bytes, x_scale, fe_w0_words, fe_w0_scales,
             (edge_sum, -11),
         )
         for s in range(-EDGE_LEAD, CHUNKS + 6):
+            if s in (-7, -7 + 1):
+                half = slice(512 * (s - -7), 512 * (s - -7) + 512)
+                acc = psa.tile([P, F1], F32, name="acc")
+                nc.tensor.matmul(acc[:], lhsT=first_row[:], rhs=brow[:, F1 + half.start : F1 + half.stop], start=True, stop=True)
+                nc.scalar.copy(out=b1[:, half], in_=acc[:])
             if s == -3:
                 bt = psa.tile([P, 8, P], BF16, name="bt", tag="acc")
                 for g in range(8):
@@ -369,13 +387,9 @@ def tile_graph_gan_pa_w4_kernel(tc, x_bytes, x_scale, fe_w0_words, fe_w0_scales,
             for stage, lag in stages:
                 if 0 <= s - lag < CHUNKS:
                     stage(s - lag)
-            for b in range(1, B):
+            for b in range(2, B):
                 first = 8 * b - EDGE_LEAD
-                if s == first - 5:
-                    node_spread(b)
-                if s == first - 4:
-                    node_quantize(b)
                 if s == first - 3:
                     node_matmul(b)
-                if s == first - 2:
+                if s == first - 3 + 1:
                     node_evacuate(b)

from contextlib import ExitStack

import concourse.mybir as mybir
from concourse.masks import make_identity

B, N, D, F1, F2 = 4, 32, 512, 512, 1024
FLOPS = 2 * 2 * B * N * D * F1 + 2 * B * N * N * F1 * F2

F32 = mybir.dt.float32
BF16 = mybir.dt.bfloat16
U32 = mybir.dt.uint32
I32 = mybir.dt.int32
U8 = mybir.dt.uint8
E4M3 = mybir.dt.float8_e4m3fn
FP8X4 = mybir.dt.float8_e4m3fn_x4
FP4X4 = mybir.dt.float4_e2m1fn_x4
ALU = mybir.AluOpType
ACT = mybir.ActivationFunctionType

P = 128
ALPHA = 0.2
CHUNKS = 32
EDGE_LEAD = 11


def tile_graph_gan_pa_w4_kernel(tc, x_bytes, x_scale, fe_w0_words, fe_w0_scales, fe_b0, fe_w1_words, fe_w1_scales, fe_b1, out):
    nc = tc.nc
    with ExitStack() as ctx:
        keep = ctx.enter_context(tc.tile_pool(name="keep", bufs=1))
        xp = ctx.enter_context(tc.tile_pool(name="xp", bufs=4))
        uvp = ctx.enter_context(tc.tile_pool(name="uvp", bufs=2))
        zp = ctx.enter_context(tc.tile_pool(name="zp", bufs=3))
        gp = ctx.enter_context(tc.tile_pool(name="gp", bufs=2))
        yp = ctx.enter_context(tc.tile_pool(name="yp", bufs=7))
        rp = ctx.enter_context(tc.tile_pool(name="rp", bufs=8))
        op = ctx.enter_context(tc.tile_pool(name="op", bufs=5))
        lrp = ctx.enter_context(tc.tile_pool(name="lrp", bufs=2))
        psz = ctx.enter_context(tc.psum_pool(name="psz", bufs=4))
        psa = ctx.enter_context(tc.psum_pool(name="psa", bufs=4))
        ctx.enter_context(tc.manual_schedule())

        xb = keep.tile([P, D], U8, name="xb", align_bytes=64)
        nc.sync.dma_start(out=xb[:], in_=x_bytes.rearrange("b n k -> (b n) k"))
        xsc = keep.tile([P, 4], F32, name="xsc")
        nc.sync.dma_start(out=xsc[:], in_=x_scale.rearrange("o q (p t) -> p (o q t)", t=4))
        w0s = keep.tile([P, 2, F1], U8, name="w0s", align_bytes=64)
        w0s_i = w0s[:].rearrange("p g n -> p (g n)").bitcast(I32)
        nc.vector.memset(w0s_i, 0)
        w1s = keep.tile([P, F2], U8, name="w1s", align_bytes=64)
        nc.vector.memset(w1s[:].bitcast(I32), 0)
        brow = keep.tile([P, F1 + F2], BF16, name="brow", align_bytes=64)
        nc.gpsimd.memset(brow[:].bitcast(I32), 0)
        first_row = keep.tile([P, P], BF16, name="first_row", align_bytes=64)
        nc.vector.memset(first_row[:], 0.0)
        nc.vector.memset(first_row[0:1, :], 1.0)
        nc.scalar.dma_start(out=brow[0:1, 0:F1], in_=fe_b0.rearrange("(o n) -> o n", o=1))
        nc.scalar.dma_start(out=brow[0:1, F1 : F1 + F2], in_=fe_b1.rearrange("(o n) -> o n", o=1))
        for q in range(4):
            nc.sync.dma_start(
                out=w0s_i.rearrange("p (g n) -> p g n", g=2)[32 * q : 32 * q + 4],
                in_=fe_w0_scales.bitcast(I32)[:, 4 * q : 4 * q + 4, :].rearrange("g r n -> r g n"),
            )
        w0 = keep.tile([P, 2, 2 * F1], U8, name="w0", align_bytes=64)
        nc.sync.dma_start(
            out=w0[:].rearrange("p g n -> p (g n)").bitcast(I32).rearrange("p (g n) -> p g n", g=2),
            in_=fe_w0_words.bitcast(I32).rearrange("g p n -> p g n"),
        )
        for q in range(4):
            nc.sync.dma_start(
                out=w1s[:].bitcast(I32)[32 * q : 32 * q + 4],
                in_=fe_w1_scales.bitcast(I32)[0, 4 * q : 4 * q + 4, :],
            )
        w1 = keep.tile([P, 2 * F2], U8, name="w1", align_bytes=64)
        nc.sync.dma_start(out=w1[:].bitcast(I32), in_=fe_w1_words.bitcast(I32)[0])
        b0 = keep.tile([P, 4, P], BF16, name="b0", align_bytes=64)
        b1 = keep.tile([P, F2], BF16, name="b1", align_bytes=64)

        zeros = keep.tile([P, 512], BF16, name="zeros", align_bytes=64)
        nc.vector.memset(zeros[:], 0.0)

        def keep_busy(n):
            idle = psa.tile([P, F1], F32, name="acc")
            for i in range(n):
                nc.tensor.matmul(idle[:], lhsT=zeros[:, 0:P], rhs=zeros[:], start=True, stop=True)

        keep_busy(4)
        b1c = keep.tile([P, 8], F32, name="b1c")
        b1a = keep.tile([P, 8], F32, name="b1a")
        warm = keep.tile([P, 1], F32, name="warm")
        nc.vector.memset(warm[:], 0.0)
        nc.scalar.activation(out=warm[:], in_=warm[:], func=ACT.Relu)

        identb = keep.tile([P, P], BF16, name="identb")
        make_identity(nc, identb[:])
        ident = keep.tile([P, P], F32, name="ident")
        make_identity(nc, ident[:])

        xw = keep.tile([P, D], BF16, name="xw", align_bytes=64)
        nc.vector.tensor_copy(out=xw[:], in_=xb[:].bitcast(E4M3))
        xt = psz.tile([P, 4, P], BF16, name="xt", tag="z")
        for t in range(4):
            nc.tensor.transpose(xt[:, t, :], xw[:].rearrange("p (k t) -> p t k", t=4)[:, t, :], identb[:])

        acc = psa.tile([P, F1], F32, name="acc")
        nc.tensor.matmul(acc[:], lhsT=first_row[:], rhs=brow[:, 0:F1], start=True, stop=True)
        nc.scalar.copy(out=b0[:], in_=acc[:].rearrange("p (k t) -> p t k", t=4))
        keep_busy(4)
        nodes = {}
        edges = {}
        grouped = {}
        codes = {}
        chunk = {}
        channel = {}

        def node_spread(b):
            xg = xp.tile([P, 4, N, 4], BF16, name="xg", align_bytes=64)
            if b == 0:
                nc.vector.tensor_tensor(
                    out=xg[:],
                    in0=xt_s[:, 0:N, :].unsqueeze(1).to_broadcast([P, 4, N, 4]),
                    in1=xsc[:].unsqueeze(1).unsqueeze(1).to_broadcast([P, 4, N, 4]),
                    op=ALU.mult,
                )
            else:
                nc.vector.tensor_copy(out=xg[:], in_=xn[:, b - 1, :, :].unsqueeze(1).to_broadcast([P, 4, N, 4]))
            nodes[b] = xg

        def node_quantize(b):
            xc = xp.tile([P, P], U32, name="xc", align_bytes=64)
            xs = xp.tile([P, P], U8, name="xs", align_bytes=64)
            nc.vector.quantize_mx(out=xc[:].bitcast(FP8X4), scales=xs[:], in_=nodes[b][:].rearrange("p d n t -> p (d n t)"))
            nodes[b] = [xc, xs]

        def node_matmul(b):
            xc, xs = nodes[b]
            for g in range(2):
                acc = psa.tile([P, F1], F32, name="acc")
                nc.tensor.matmul_mx(
                    out=acc[:], lhsT=xc[:].bitcast(FP8X4), lhsT_scale=xs[:], rhs=w0[:, g, :].bitcast(FP4X4), rhs_scale=w0s[:, g, :], start=True, stop=True
                )
                nodes[b].append(acc)

        def node_evacuate(b):
            u = uvp.tile([P, 4, P], F32, name="u", align_bytes=64)
            if b in (9,):
                ua = uvp.tile([P, 4, P], F32, name="ua", align_bytes=64)
                nc.scalar.copy(out=ua[:], in_=nodes[b][2][:].rearrange("p (k t) -> p t k", t=4))
                nc.gpsimd.tensor_tensor(out=u[:], in0=ua[:], in1=b0[:], op=ALU.add)
            else:
                nc.vector.tensor_tensor(out=u[:], in0=nodes[b][2][:].rearrange("p (k t) -> p t k", t=4), in1=b0[:], op=ALU.add)
            v = uvp.tile([P, 4, P], F32, name="v", align_bytes=64)
            nc.scalar.copy(out=v[:], in_=nodes[b][3][:].rearrange("p (k t) -> p t k", t=4))
            nodes[b] += [u, v]

        def edge_sum(k):
            u, v = nodes[k // 8][4:6]
            c = k % 8
            z = psz.tile([P, 4, P], F32, name="z", tag="z")
            for t in range(4):
                nc.tensor.matmul(z[:, t, :], lhsT=u[:, t, :], rhs=pi_u[:], is_transpose=True, start=True, stop=False)
                nc.tensor.matmul(z[:, t, :], lhsT=v[:, t, :], rhs=pi_v[:, c, :, :].rearrange("p h e -> p (h e)"), is_transpose=True, start=False, stop=True)
            edges[k] = z

        def edge_scale(k):
            zs = zp.tile([P, P, 4], F32, name="zs")
            nc.scalar.mul(out=zs[:], in_=edges[k][:].rearrange("p t e -> p e t"), mul=ALPHA)
            edges[k] = (edges[k], zs)

        def edge_max(k):
            b, c = divmod(k, 8)
            if c == 0:
                grouped[b] = gp.tile([P, 76, 64], BF16, name="e1", align_bytes=64)
            z, zs = edges.pop(k)
            z = z[:].rearrange("p t (h r) -> p h r t", h=8)
            zs = zs[:].rearrange("p (h r) t -> p h r t", h=8)
            step = [(7 if c >> i & 1 else 9) << i for i in range(3)]
            if step[1] == 2 * step[0]:
                runs = [(0, c, 2, step[2], 4, step[0])]
            elif step[2] == 2 * step[1]:
                runs = [(0, c, 4, step[1], 2, step[0])]
            else:
                runs = [(4 * h, c + h * step[2], 2, step[1], 2, step[0]) for h in range(2)]
            for h, first, na, sa, nb, sb in runs:
                dst = grouped[b][:, first : first + na * sa, :].rearrange("p (a x) (r t) -> p a x r t", a=na, t=4)
                nc.vector.tensor_tensor(
                    out=dst[:, :, 0 : (nb - 1) * sb + 1 : sb, :, :],
                    in0=z[:, h : h + na * nb, :, :].rearrange("p (a x) r t -> p a x r t", a=na),
                    in1=zs[:, h : h + na * nb, :, :].rearrange("p (a x) r t -> p a x r t", a=na),
                    op=ALU.max,
                )

        def edge_quantize(k):
            b, c = divmod(k, 8)
            if c < 7:
                return
            e1 = grouped[b][:].rearrange("p i e -> p (i e)")
            for hf in range(2):
                ec = gp.tile([P, 512], U32, name="ec%d" % hf, align_bytes=64)
                es = gp.tile([P, 512], U8, name="es%d" % hf, align_bytes=64)
                nc.vector.quantize_mx(out=ec[:].bitcast(FP8X4), scales=es[:], in_=e1[:, 2048 * hf : 2048 * (hf + 1)])
                codes[2 * b + hf] = (ec, es)

        def widths(s):
            if s < 24:
                return 768, 0
            if s < 31:
                return 512, 0
            return 256, 256

        def groups(s):
            wg, wf = widths(s)
            return list(range((wg + wf) // P, 8))

        def out_matmul(s):
            ec, es = codes[s // 4]
            cols = slice(P * (s % 4), P * (s % 4) + P)
            wg, wf = widths(s)
            chunk[s] = {}
            for f0 in range(0, wg + wf, 512):
                n = min(512, wg + wf - f0)
                acc = psa.tile([P, F1], F32, name="acc")
                nc.tensor.matmul_mx(
                    out=acc[:, 0:n],
                    lhsT=ec[:, cols].bitcast(FP8X4),
                    lhsT_scale=es[:, cols],
                    rhs=w1[:, 2 * f0 : 2 * (f0 + n)].bitcast(FP4X4),
                    rhs_scale=w1s[:, f0 : f0 + n],
                    start=True,
                    stop=True,
                )
                chunk[s][f0] = (acc, n)

        def out_add(s, f0):
            if f0 in chunk[s]:
                acc, n = chunk[s][f0]
                nc.vector.tensor_tensor(out=chunk[s]["y"][:, f0 : f0 + n], in0=acc[:, 0:n], in1=b1[:, f0 : f0 + n], op=ALU.add)

        def out_add_first(s):
            chunk[s]["y"] = yp.tile([P, F2], F32, name="y")
            out_add(s, 0)

        def out_add_second(s):
            out_add(s, 512)

        def out_relu(s):
            wg, wf = widths(s)
            r = rp.tile([P, F2], F32, name="r")
            nc.scalar.activation(out=r[:, 0:wg], in_=chunk[s]["y"][:, 0:wg], func=ACT.Relu, scale=ALPHA - 1.0)
            chunk[s]["r"] = r

        def out_tile(s):
            if "o" not in chunk[s]:
                chunk[s]["o"] = op.tile([P, F2], F32, name="o")
            return chunk[s]["o"]

        def out_gpsimd(s):
            wg, wf = widths(s)
            o = out_tile(s)
            nc.gpsimd.tensor_tensor(out=o[:, 0:wg], in0=chunk[s]["y"][:, 0:wg], in1=chunk[s]["r"][:, 0:wg], op=ALU.add)

        def out_vector(s):
            wg, wf = widths(s)
            if wf:
                o = out_tile(s)
                y = chunk[s]["y"][:, wg : wg + wf]
                nc.vector.scalar_tensor_tensor(out=o[:, wg : wg + wf], in0=y, scalar=ALPHA, in1=y, op0=ALU.mult, op1=ALU.max)

        def channel_work(s):
            q, i = divmod(s, 4)
            return [(q, g) for n, g in enumerate(groups(s)) if n % 2 == i]

        def channel_matmul(s):
            for q, g in channel_work(s):
                ec, es = codes[q]
                acc = psa.tile([P, F1], F32, name="acc")
                nc.tensor.matmul_mx(
                    out=acc[:],
                    lhsT=w1[:, 256 * g : 256 * (g + 1)].bitcast(FP4X4),
                    lhsT_scale=w1s[:, P * g : P * (g + 1)],
                    rhs=ec[:].bitcast(FP8X4),
                    rhs_scale=es[:],
                    start=True,
                    stop=True,
                )
                channel[q, g] = acc

        def channel_scale(s):
            for q, g in channel_work(s):
                ys = zp.tile([P, 512], F32, name="ys")
                nc.scalar.activation(out=ys[:], in_=channel[q, g][:], func=ACT.Identity, scale=ALPHA, bias=b1a[:, g : g + 1])
                channel[q, g] = (channel[q, g], ys)

        def channel_max(s):
            for q, g in channel_work(s):
                acc, ys = channel[q, g]
                lr = lrp.tile([P, 512], F32, name="lr%d" % (g % 4))
                nc.vector.scalar_tensor_tensor(out=lr[:], in0=acc[:], scalar=b1c[:, g : g + 1], in1=ys[:], op0=ALU.add, op1=ALU.max)
                channel[q, g] = lr

        def out_transpose(s):
            cols = slice(P * (s % 4), P * (s % 4) + P)
            tr = psz.tile([P, 4, P], F32, name="tr", tag="z")
            for i, g in enumerate(groups(s)):
                nc.tensor.transpose(tr[:, i, :], channel[s // 4, g][:, cols], ident[:])
            chunk[s]["tr"] = tr

        def out_copy(s):
            gs = groups(s)
            o = out_tile(s)
            tr = chunk[s]["tr"][:, 0 : len(gs), :].rearrange("p i e -> p (i e)")
            if s % 4 == 1:
                nc.vector.tensor_copy(out=o[:, P * gs[0] : F2], in_=tr)
            else:
                nc.scalar.copy(out=o[:, P * gs[0] : F2], in_=tr)

        def out_store(s):
            o = chunk[s]["o"]
            b, h = divmod(s, 8)
            dst = out[b, 4 * h : 4 * h + 4].rearrange("l j f -> j l f")
            wg = widths(s)[0] if s == CHUNKS - 1 else 0
            nc.sync.dma_start(out=dst[:, :, wg:F2], in_=o[:, wg:F2])
            if wg:
                nc.sync.dma_start(out=dst[:, :, 0:wg], in_=o[:, 0:wg])

        xt_s = xt[:].rearrange("p t m -> p m t")
        node_spread(0)
        xn = keep.tile([P, 3, N, 4], BF16, name="xn", align_bytes=64)
        nc.vector.tensor_tensor(
            out=xn[:].rearrange("p b n t -> p (b n) t"), in0=xt_s[:, N : 4 * N, :], in1=xsc[:].unsqueeze(1).to_broadcast([P, 3 * N, 4]), op=ALU.mult
        )
        node_quantize(0)
        node_spread(1)
        pi_u = keep.tile([P, P], F32, name="pi_u", align_bytes=64)
        nc.vector.tensor_copy(
            out=pi_u[:].rearrange("p (h j l) -> p h j l", h=8, j=4), in_=ident[:].rearrange("p (j h l) -> p h j l", h=8, j=4)
        )
        node_quantize(1)
        pi_v = keep.tile([P, 8, 8, 16], F32, name="pi_v", align_bytes=64)
        nc.vector.tensor_copy(
            out=pi_v[:, 0, :, :].rearrange("p h (j l) -> p h j l", j=4), in_=ident[:].rearrange("p (l h j) -> p h j l", h=8, j=4)
        )
        node_matmul(0)
        node_matmul(1)
        node_evacuate(0)
        for w in (1, 2, 4):
            for half in range(2):
                eng = nc.gpsimd if w == 4 else nc.vector
                eng.tensor_copy(
                    out=pi_v[:, w : 2 * w, :, :].rearrange("p c (a x b) e -> p c a x (b e)", x=2, b=w)[:, :, :, half, :],
                    in_=pi_v[:, 0:w, :, :].rearrange("p c (a x b) e -> p c a x (b e)", x=2, b=w)[:, :, :, 1 - half, :],
                )
        node_evacuate(1)
        node_spread(2)
        node_spread(3)
        node_quantize(2)
        node_quantize(3)
        stages = (
            (out_vector, 3),
            (channel_max, 2),
            (channel_scale, 1),
            (out_matmul, 0),
            (channel_matmul, 0),
            (edge_quantize, -8),
            (out_add_first, 1),
            (out_copy, 4),
            (out_gpsimd, 4),
            (edge_max, -9),
            (out_relu, 2),
            (out_store, 4),
            (out_transpose, 3),
            (out_add_second, 1),
            (edge_scale, -10),
            (edge_sum, -11),
        )
        for s in range(-EDGE_LEAD, CHUNKS + 6):
            if s in (-7, -7 + 1):
                half = slice(512 * (s - -7), 512 * (s - -7) + 512)
                acc = psa.tile([P, F1], F32, name="acc")
                nc.tensor.matmul(acc[:], lhsT=first_row[:], rhs=brow[:, F1 + half.start : F1 + half.stop], start=True, stop=True)
                nc.scalar.copy(out=b1[:, half], in_=acc[:])
            if s == -3:
                bt = psa.tile([P, 8, P], BF16, name="bt", tag="acc")
                for g in range(8):
                    nc.tensor.transpose(bt[:, g, :], b1[:, P * g : P * (g + 1)], identb[:])
                nc.vector.tensor_copy(out=b1c[:], in_=bt[:, :, 0])
                nc.vector.tensor_scalar(out=b1a[:], in0=bt[:, :, 0], scalar1=ALPHA, scalar2=None, op0=ALU.mult)
            for stage, lag in stages:
                if 0 <= s - lag < CHUNKS:
                    stage(s - lag)
            for b in range(2, B):
                first = 8 * b - EDGE_LEAD
                if s == first - 3:
                    node_matmul(b)
                if s == first - 3 + 1:
                    node_evacuate(b)
